import numpy as np
import ml_dtypes


def mxq(x, axis, fmt="e4m3"):
    dtype, down = {"e4m3": (ml_dtypes.float8_e4m3fn, 7), "e5m2": (ml_dtypes.float8_e5m2, 14)}[fmt]
    v = np.moveaxis(np.asarray(x, np.float32).astype(ml_dtypes.bfloat16).astype(np.float64), axis, -1)
    blocks = v.reshape(v.shape[:-1] + (-1, 32))
    amax = np.abs(blocks).max(-1, keepdims=True)
    byte = np.maximum(np.where(amax > 0, np.frexp(amax)[1] - 1 + 127, 0) - down, 1)
    scale = np.exp2(byte - 127.0)
    codes = (blocks / scale).astype(np.float32).astype(dtype).astype(np.float64)
    return np.moveaxis((codes * scale).reshape(v.shape), -1, axis)


WIDE = False


def mx_kscale(k):
    if not WIDE:
        return np.ones(k)
    levels = np.array([10, -10, 5, -5, 0])
    if k % 512:
        return np.exp2(np.random.permutation(np.resize(levels, k // 32))).repeat(32)
    a = np.empty((k // 512, 16))
    for p in range(k // 512):
        a[p, :8] = np.random.permutation(np.resize(levels, 8))
        for g in range(8):
            far = levels[np.abs(levels - a[p, g]) >= 10]
            a[p, g + 8] = far[np.random.randint(len(far))]
    return np.exp2(a.ravel()).repeat(32)


BF16 = ml_dtypes.bfloat16


def bf(x):
    return np.asarray(x, np.float32).astype(BF16)


def f64(x):
    return np.asarray(x).astype(np.float64)


B, NV, S, D, H = 2, 8, 512, 2048, 16
HD = D // H


def setup_inputs():
    s, t = mx_kscale(D), mx_kscale(D)
    return {"x": bf(np.random.standard_normal((B * NV, S, D)) * s),
            "scores": bf(np.random.standard_normal((B, NV, NV, H, S)) * 1.4),
            "Wv": bf(np.random.standard_normal((D, D)) / np.sqrt(D) / s[:, None] * t),
            "bv": bf(np.random.standard_normal(D) * 0.3 * t),
            "Wo": bf(np.random.standard_normal((D, D)) / np.sqrt(D) / t[:, None]),
            "bo": bf(np.random.standard_normal(D) * 0.3)}


def reference(x, scores, Wv, bv, Wo, bo):
    v = (mxq(f64(x), 2, "e4m3") @ mxq(f64(Wv), 0, "e4m3")) + f64(bv)
    v = v.reshape(B, NV, S, H, HD).transpose(0, 1, 3, 2, 4)
    sc = f64(scores)
    e = np.exp(sc - sc.max(2, keepdims=True))
    w = e / e.sum(2, keepdims=True)
    mixed = np.zeros((B, NV, H, S, HD))
    for j in range(NV):
        mixed = mixed + w[:, :, j, :, :, None] * v[:, j][:, None]
    mixed = mixed.transpose(0, 1, 3, 2, 4).reshape(B * NV, S, D)
    return (mxq(mixed, 2, "e4m3") @ mxq(f64(Wo), 0, "e4m3")) + f64(bo)

@@ -1,0 +1,359 @@
+from contextlib import ExitStack
+
+import concourse.mybir as mybir
+from concourse.masks import make_identity
+
+F32 = mybir.dt.float32
+BF16 = mybir.dt.bfloat16
+U32 = mybir.dt.uint32
+U8 = mybir.dt.uint8
+FP8X4 = mybir.dt.float8_e4m3fn_x4
+ALU = mybir.AluOpType
+ACTF = mybir.ActivationFunctionType
+AX = mybir.AxisListType
+
+B, NV, S, D, H = 2, 8, 512, 2048, 16
+P = 128
+SPT = P // NV
+NSB = S // SPT
+NT = B * NSB
+NG = D // 512
+NQ = D // 512
+CH = 128
+TPC = CH // SPT
+NCH = B * S // CH
+
+FLOPS = 2 * 2 * B * NV * S * D * D + 2 * B * NV * NV * S * D
+
+LAG = 5
+W_AHEAD = 2
+W_PER_ITER = 4
+RAW_BUFS = 5
+
+
+def tile_crossviewattention_pa_l_kernel(tc, x, scores, Wv, bv, Wo, bo, out):
+    nc = tc.nc
+    with ExitStack() as ctx:
+        const = ctx.enter_context(tc.tile_pool(name="const", bufs=1))
+        work = ctx.enter_context(tc.tile_pool(name="work", bufs=2))
+        psum = ctx.enter_context(tc.psum_pool(name="psum", bufs=2))
+        ctx.enter_context(tc.manual_schedule())
+
+        warm = const.tile([P, 1], F32, name="warm")
+        nc.vector.memset(warm[:], 0.0)
+        nc.scalar.activation(out=warm[:], in_=warm[:], func=ACTF.Exp)
+
+        ident = const.tile([P, P], F32, name="ident")
+        make_identity(nc, ident[:])
+        mask = const.tile([P, SPT], F32, name="mask")
+        nc.vector.tensor_reduce(
+            out=mask[:], in_=ident[:].rearrange("p (s v) -> p s v", v=NV), axis=AX.X, op=ALU.add
+        )
+
+        wv_c = const.tile([P, NG * D], U32, name="wv_c", align_bytes=64)
+        wv_s = const.tile([P, NG * D], U8, name="wv_s", align_bytes=64)
+        wo_c = const.tile([P, NG * D], U32, name="wo_c", align_bytes=64)
+        wo_s = const.tile([P, NG * D], U8, name="wo_s", align_bytes=64)
+        bv_bc = const.tile([P, D], BF16, name="bv_bc")
+        bo_bc = const.tile([P, D], BF16, name="bo_bc")
+
+        xraw = {}
+        xsort = {}
+        xq = {}
+        vsb = {}
+        wmix = {}
+        w2ps = {}
+        mbf = {}
+        mq = {}
+        sct = {}
+        sm = {}
+        wch = {}
+
+        def load_scores(b):
+            t = work.tile([P, NV, S], BF16, tag="sc", bufs=1, name="sc")
+            for i in range(NV):
+                nc.sync.dma_start(out=t[i:P:NV, :, :], in_=scores[b, i].rearrange("j h s -> h j s"))
+            sct[b] = t
+
+        def load_x(n):
+            b, sb = divmod(n, NSB)
+            t = work.tile([P, D], BF16, tag="raw", bufs=RAW_BUFS, name="xraw")
+            for j in range(NV):
+                nc.sync.dma_start(out=t[j:P:NV, :], in_=x[b * NV + j, sb * SPT:(sb + 1) * SPT, :])
+            xraw[n] = t
+
+        wchunks = []
+        for (W, wc, ws) in ((Wv, wv_c, wv_s), (Wo, wo_c, wo_s)):
+            for q in range(NQ):
+                for g in range(NG):
+                    wchunks.append((W, wc, ws, g, q))
+        wraw = {}
+        wpend = [None]
+
+        def w_load(c):
+            W, wc, ws, g, q = wchunks[c]
+            t = work.tile([P, D], BF16, tag="raw", bufs=RAW_BUFS, name="wraw")
+            nc.sync.dma_start(
+                out=t[:].rearrange("p (j c) -> p j c", j=4),
+                in_=W.rearrange("(g p j) c -> g p j c", g=NG, j=4)[g, :, :, q * 512:(q + 1) * 512],
+            )
+            wraw[c] = t
+
+        def w_flush():
+            if wpend[0] is not None:
+                gt, c = wpend[0]
+                W, wc, ws, g, q = wchunks[c]
+                lo = g * D + q * 512
+                nc.vector.quantize_mx(
+                    out=wc[:, lo:lo + 512].bitcast(FP8X4), scales=ws[:, lo:lo + 512], in_=gt[:]
+                )
+            wpend[0] = None
+
+        def w_step(c):
+            gt = work.tile([P, D], BF16, tag="grp", bufs=3, name="wgrp", align_bytes=64)
+            o = gt[:].rearrange("p (c j) -> p c j", j=4)
+            i = wraw[c][:].rearrange("p (j c) -> p c j", j=4)
+            if c % 2 == 0:
+                nc.vector.tensor_copy(out=o, in_=i)
+            else:
+                nc.scalar.copy(out=o, in_=i)
+            if c + W_AHEAD < len(wchunks):
+                w_load(c + W_AHEAD)
+            w_flush()
+            wpend[0] = (gt, c)
+
+        def softmax_op(c, op):
+            b, qc = divmod(c, S // CH)
+            if op == 0:
+                src = sct[b][:, :, qc * CH:(qc + 1) * CH].rearrange("p j s -> p s j")
+                mxv = work.tile([P, CH], F32, tag="mxv", bufs=1, name="mxv")
+                nc.vector.tensor_reduce(out=mxv[:], in_=src, axis=AX.X, op=ALU.max)
+                sm[(c, "mx")] = mxv
+            elif op == 1:
+                src = sct[b][:, :, qc * CH:(qc + 1) * CH].rearrange("p j s -> p s j")
+                d = work.tile([P, CH, NV], F32, tag="d", bufs=1, name="d")
+                nc.vector.tensor_tensor(
+                    out=d[:], in0=src, in1=sm[(c, "mx")][:].unsqueeze(2).to_broadcast([P, CH, NV]),
+                    op=ALU.subtract,
+                )
+                sm[(c, "d")] = d
+            elif op == 2:
+                d = sm[(c, "d")]
+                nc.scalar.activation(out=d[:], in_=d[:], func=ACTF.Exp)
+            elif op == 3:
+                z = work.tile([P, CH], F32, tag="z", bufs=1, name="z")
+                nc.vector.tensor_reduce(out=z[:], in_=sm[(c, "d")][:], axis=AX.X, op=ALU.add)
+                sm[(c, "z")] = z
+            elif op == 4:
+                r = work.tile([P, CH], F32, tag="r", bufs=1, name="r")
+                nc.vector.reciprocal(out=r[:], in_=sm[(c, "z")][:])
+                sm[(c, "r")] = r
+            elif op == 5:
+                w = work.tile([P, CH, NV], F32, tag="w", bufs=2, name="w")
+                nc.vector.tensor_tensor(
+                    out=w[:], in0=sm[(c, "d")][:],
+                    in1=sm[(c, "r")][:].unsqueeze(2).to_broadcast([P, CH, NV]), op=ALU.mult,
+                )
+                wch[c] = w
+
+        def to_grouped(src):
+            words = src[:].bitcast(F32)
+            grp = work.tile([P, D], BF16, tag="grp", bufs=3, name="grp", align_bytes=64)
+            gw = grp[:].bitcast(F32).rearrange("p (g r u) -> p g r u", g=NG, u=2)
+            for half in range(2):
+                ps = psum.tile([P, 512], F32, tag="tr", bufs=3, name="trps")
+                for gl in range(2):
+                    g = 2 * half + gl
+                    for u in range(2):
+                        col = (2 * gl + u) * P
+                        lo = 256 * g + P * u
+                        nc.tensor.transpose(ps[:, col:col + P], words[:, lo:lo + P], ident[:])
+                nc.scalar.copy(
+                    out=gw[:, 2 * half:2 * half + 2, :, :],
+                    in_=ps[:].rearrange("p (g u r) -> p g r u", g=2, u=2),
+                )
+            return grp
+
+        def quantize(grp, tag, bufs):
+            codes = work.tile([P, 512], U32, tag=tag + "c", bufs=bufs, name=tag + "c", align_bytes=64)
+            scl = work.tile([P, 512], U8, tag=tag + "s", bufs=bufs, name=tag + "s", align_bytes=64)
+            nc.vector.quantize_mx(out=codes[:].bitcast(FP8X4), scales=scl[:], in_=grp[:])
+            return (codes, scl)
+
+        def mx_stage(opnd, wc, ws, consume):
+            codes, scl = opnd
+            for q in range(NQ):
+                acc = psum.tile([P, 512], F32, tag="acc", bufs=3, name="acc")
+                for g in range(NG):
+                    lo = g * D + q * 512
+                    nc.tensor.matmul_mx(
+                        out=acc[:],
+                        lhsT=codes[:, g * P:(g + 1) * P].bitcast(FP8X4),
+                        lhsT_scale=scl[:, g * P:(g + 1) * P],
+                        rhs=wc[:, lo:lo + 512].bitcast(FP8X4),
+                        rhs_scale=ws[:, lo:lo + 512],
+                        start=(g == 0),
+                        stop=(g == NG - 1),
+                    )
+                consume(q, acc)
+
+        def sort_x(n):
+            t = work.tile([P, D], BF16, tag="xs", bufs=2, name="xs")
+            nc.scalar.copy(
+                out=t[:].bitcast(F32).rearrange("p (g u m) -> p g u m", g=NG, u=2),
+                in_=xraw[n][:].bitcast(F32).rearrange("p (g m u) -> p g u m", g=NG, u=2),
+            )
+            xsort[n] = t
+
+        def transp_x(n):
+            xq[n] = to_grouped(xsort[n])
+
+        def quant_x(n):
+            xq[n] = quantize(xq[n], "xq", 3)
+
+        def stage1(n):
+            v = work.tile([P, D], F32, tag="v", bufs=2, name="v")
+            vsb[n] = v
+
+            def consume(q, acc):
+                nc.scalar.copy(out=v[:, q * 512:(q + 1) * 512], in_=acc[:])
+
+            mx_stage(xq[n], wv_c, wv_s, consume)
+
+        def w2t(n):
+            c, sl = divmod(n, TPC)
+            ps = psum.tile([P, 512], F32, tag="tr", bufs=3, name="w2ps")
+            nc.tensor.transpose(
+                ps[:, 0:P], wch[c][:].rearrange("p s j -> p (s j)")[:, sl * P:(sl + 1) * P], ident[:]
+            )
+            w2ps[n] = ps
+
+        def build_wmix(n):
+            wm = work.tile([P, D], F32, tag="wm", bufs=2, name="wm")
+            shp = [P, H, SPT, NV]
+            nc.vector.tensor_tensor(
+                out=wm[:].rearrange("p (h s i) -> p h s i", h=H, s=SPT),
+                in0=w2ps[n][:, 0:P].rearrange("p (h i) -> p h i", i=NV).unsqueeze(2).to_broadcast(shp),
+                in1=mask[:].unsqueeze(1).unsqueeze(3).to_broadcast(shp),
+                op=ALU.mult,
+            )
+            wmix[n] = wm
+
+        def mix(n, after_first):
+            mb = work.tile([P, D], BF16, tag="mb", bufs=2, name="mb")
+            v = vsb[n]
+            wm = wmix[n]
+            for q in range(NQ):
+                ps = psum.tile([P, 512], F32, tag="mx", bufs=2, name="mxps")
+                for hl in range(4):
+                    h = 4 * q + hl
+                    nc.tensor.matmul(
+                        out=ps[:, hl * P:(hl + 1) * P],
+                        lhsT=wm[:, h * P:(h + 1) * P],
+                        rhs=v[:, h * P:(h + 1) * P],
+                        start=True,
+                        stop=True,
+                    )
+                nc.vector.tensor_tensor(
+                    out=mb[:, q * 512:(q + 1) * 512].rearrange("p (u m e) -> p m u e", u=2, e=2),
+                    in0=ps[:].rearrange("p (m u e) -> p m u e", u=2, e=2),
+                    in1=bv_bc[:, q * 512:(q + 1) * 512].rearrange("p (m u e) -> p m u e", u=2, e=2),
+                    op=ALU.add,
+                )
+                if q == 0:
+                    after_first()
+            mbf[n] = mb
+
+        def transp_m(n):
+            mq[n] = to_grouped(mbf[n])
+
+        def quant_m(n):
+            mq[n] = quantize(mq[n], "mq", LAG + 1)
+
+        def stage2(n, after_first):
+            b, sb = divmod(n, NSB)
+            y = work.tile([P, D], F32, tag="y", bufs=2, name="y")
+
+            def consume(q, acc):
+                nc.vector.tensor_tensor(
+                    out=y[:, q * 512:(q + 1) * 512], in0=acc[:], in1=bo_bc[:, q * 512:(q + 1) * 512],
+                    op=ALU.add,
+                )
+                if q == 0:
+                    after_first()
+
+            mx_stage(mq[n], wo_c, wo_s, consume)
+            for i in range(NV):
+                nc.sync.dma_start(out=out[b * NV + i, sb * SPT:(sb + 1) * SPT, :], in_=y[i:P:NV, :])
+
+        load_scores(0)
+        load_x(0)
+        for c in range(W_AHEAD):
+            w_load(c)
+        load_x(1)
+        sort_x(0)
+        transp_x(0)
+        quant_x(0)
+        for op in range(6):
+            softmax_op(0, op)
+        w2t(0)
+        for c in range(NQ * NG):
+            w_step(c)
+            if c == 3:
+                sort_x(1)
+                transp_x(1)
+                quant_x(1)
+                load_x(2)
+            if c == 7:
+                load_x(3)
+                nc.sync.dma_start(out=bv_bc[:], in_=bv.partition_broadcast(P))
+            if c == 9:
+                sort_x(2)
+            if c == 11:
+                nc.sync.dma_start(out=bo_bc[:], in_=bo.partition_broadcast(P))
+        w_flush()
+
+        def nothing():
+            return None
+
+        wnext = [NQ * NG]
+        for k in range(NT + LAG):
+            if k < NT:
+                build_wmix(k)
+                stage1(k)
+                cnext = k // TPC + 1
+                if cnext < NCH:
+                    if k % TPC < 6:
+                        softmax_op(cnext, k % TPC)
+                    if cnext == S // CH - 1 and k % TPC == 2:
+                        load_scores(1)
+            if 1 <= k <= NT:
+                transp_m(k - 1)
+            if k < NT:
+                if k >= 1:
+                    mix(k, lambda: quant_m(k - 1))
+                else:
+                    mix(k, nothing)
+            elif k == NT:
+                quant_m(k - 1)
+            for rep in range(W_PER_ITER):
+                if wnext[0] < len(wchunks):
+                    w_step(wnext[0])
+                    wnext[0] += 1
+                    if wnext[0] == len(wchunks):
+                        w_flush()
+            if k + 2 < NT:
+                transp_x(k + 2)
+            if k + 1 < NT:
+                w2t(k + 1)
+            if k + 3 < NT:
+                sort_x(k + 3)
+            if k + 4 < NT:
+                load_x(k + 4)
+            if k >= LAG:
+                if k + 2 < NT:
+                    stage2(k - LAG, lambda: quant_x(k + 2))
+                else:
+                    stage2(k - LAG, nothing)
+            elif k + 2 < NT:
+                quant_x(k + 2)

@@ -212,11 +212,14 @@ def tile_crossviewattention_pa_l_kernel(tc, x, scores, Wv, bv, Wo, bo, out):
             xq[n] = quantize(xq[n], "xq", 3)
 
         def stage1(n):
-            v = work.tile([P, D], F32, tag="v", bufs=2, name="v")
-            vsb[n] = v
+            vh = work.tile([P, D], BF16, tag="vh", bufs=2, name="vh")
+            vl = work.tile([P, D], BF16, tag="vl", bufs=2, name="vl")
+            vsb[n] = (vh, vl)
 
             def consume(q, acc):
-                nc.scalar.copy(out=v[:, q * 512:(q + 1) * 512], in_=acc[:])
+                sl = slice(q * 512, (q + 1) * 512)
+                nc.scalar.copy(out=vh[:, sl], in_=acc[:])
+                nc.vector.tensor_tensor(out=vl[:, sl], in0=acc[:], in1=vh[:, sl], op=ALU.subtract)
 
             mx_stage(xq[n], wv_c, wv_s, consume)
 
@@ -226,34 +229,36 @@ def tile_crossviewattention_pa_l_kernel(tc, x, scores, Wv, bv, Wo, bo, out):
             nc.tensor.transpose(
                 ps[:, 0:P], wch[c][:].rearrange("p s j -> p (s j)")[:, sl * P:(sl + 1) * P], ident[:]
             )
-            w2ps[n] = ps
+            hl = work.tile([P, 2 * P], BF16, tag="w2hl", bufs=2, name="w2hl")
+            nc.scalar.copy(out=hl[:, 0:P], in_=ps[:, 0:P])
+            w2ps[n] = (ps, hl)
 
         def build_wmix(n):
-            wm = work.tile([P, D], F32, tag="wm", bufs=2, name="wm")
-            shp = [P, H, SPT, NV]
-            nc.vector.tensor_tensor(
-                out=wm[:].rearrange("p (h s i) -> p h s i", h=H, s=SPT),
-                in0=w2ps[n][:, 0:P].rearrange("p (h i) -> p h i", i=NV).unsqueeze(2).to_broadcast(shp),
-                in1=mask[:].unsqueeze(1).unsqueeze(3).to_broadcast(shp),
-                op=ALU.mult,
-            )
+            ps, hl = w2ps[n]
+            nc.vector.tensor_tensor(out=hl[:, P:2 * P], in0=ps[:, 0:P], in1=hl[:, 0:P], op=ALU.subtract)
+            wm = work.tile([P, 2 * D], BF16, tag="wm", bufs=2, name="wm")
+            wmv = wm[:].rearrange("p (a s i) -> p a s i", s=SPT, i=NV)
+            src = hl[:].rearrange("p (a i) -> p a i", i=NV)
+            for s in range(SPT):
+                nc.vector.tensor_scalar(
+                    out=wmv[:, :, s, :], in0=src, scalar1=mask[:, s:s + 1], scalar2=None, op0=ALU.mult
+                )
             wmix[n] = wm
 
         def mix(n, after_first):
             mb = work.tile([P, D], BF16, tag="mb", bufs=2, name="mb")
-            v = vsb[n]
+            vh, vl = vsb[n]
             wm = wmix[n]
             for q in range(NQ):
                 ps = psum.tile([P, 512], F32, tag="mx", bufs=2, name="mxps")
                 for hl in range(4):
                     h = 4 * q + hl
-                    nc.tensor.matmul(
-                        out=ps[:, hl * P:(hl + 1) * P],
-                        lhsT=wm[:, h * P:(h + 1) * P],
-                        rhs=v[:, h * P:(h + 1) * P],
-                        start=True,
-                        stop=True,
-                    )
+                    o = ps[:, hl * P:(hl + 1) * P]
+                    hs = slice(h * P, (h + 1) * P)
+                    ls = slice(D + h * P, D + (h + 1) * P)
+                    nc.tensor.matmul(out=o, lhsT=wm[:, hs], rhs=vh[:, hs], start=True, stop=False)
+                    nc.tensor.matmul(out=o, lhsT=wm[:, hs], rhs=vl[:, hs], start=False, stop=False)
+                    nc.tensor.matmul(out=o, lhsT=wm[:, ls], rhs=vh[:, hs], start=False, stop=True)
                 nc.vector.tensor_tensor(
                     out=mb[:, q * 512:(q + 1) * 512].rearrange("p (u m e) -> p m u e", u=2, e=2),
                     in0=ps[:].rearrange("p (m u e) -> p m u e", u=2, e=2),

@@ -54,7 +54,9 @@ def tile_crossviewattention_pa_l_kernel(tc, x, scores, Wv, bv, Wo, bo, out):
         wv_s = const.tile([P, NG * D], U8, name="wv_s", align_bytes=64)
         wo_c = const.tile([P, NG * D], U32, name="wo_c", align_bytes=64)
         wo_s = const.tile([P, NG * D], U8, name="wo_s", align_bytes=64)
-        bv_bc = const.tile([P, D], BF16, name="bv_bc")
+        bv_rows = const.tile([P, P], BF16, name="bv_rows")
+        bv_f = const.tile([P, P], F32, name="bv_f")
+        bvT = const.tile([P, H], F32, name="bvT")
         bo_bc = const.tile([P, D], BF16, name="bo_bc")
 
         xraw = {}
@@ -63,7 +65,8 @@ def tile_crossviewattention_pa_l_kernel(tc, x, scores, Wv, bv, Wo, bo, out):
         vsb = {}
         wmix = {}
         w2ps = {}
-        mbf = {}
+        mtl = {}
+        g0l = {}
         mq = {}
         sct = {}
         sm = {}
@@ -161,7 +164,7 @@ def tile_crossviewattention_pa_l_kernel(tc, x, scores, Wv, bv, Wo, bo, out):
             grp = work.tile([P, D], BF16, tag="grp", bufs=3, name="grp", align_bytes=64)
             gw = grp[:].bitcast(F32).rearrange("p (g r u) -> p g r u", g=NG, u=2)
             for half in range(2):
-                ps = psum.tile([P, 512], F32, tag="tr", bufs=3, name="trps")
+                ps = psum.tile([P, 512], F32, tag="tr", bufs=2, name="trps")
                 for gl in range(2):
                     g = 2 * half + gl
                     for u in range(2):
@@ -212,65 +215,80 @@ def tile_crossviewattention_pa_l_kernel(tc, x, scores, Wv, bv, Wo, bo, out):
             xq[n] = quantize(xq[n], "xq", 3)
 
         def stage1(n):
-            vh = work.tile([P, D], BF16, tag="vh", bufs=2, name="vh")
-            vl = work.tile([P, D], BF16, tag="vl", bufs=2, name="vl")
-            vsb[n] = (vh, vl)
+            v = work.tile([P, D], F32, tag="v", bufs=2, name="v")
+            vsb[n] = v
 
             def consume(q, acc):
-                sl = slice(q * 512, (q + 1) * 512)
-                nc.scalar.copy(out=vh[:, sl], in_=acc[:])
-                nc.vector.tensor_tensor(out=vl[:, sl], in0=acc[:], in1=vh[:, sl], op=ALU.subtract)
+                nc.scalar.copy(out=v[:, q * 512:(q + 1) * 512], in_=acc[:])
 
             mx_stage(xq[n], wv_c, wv_s, consume)
 
         def w2t(n):
             c, sl = divmod(n, TPC)
-            ps = psum.tile([P, 512], F32, tag="tr", bufs=3, name="w2ps")
-            nc.tensor.transpose(
-                ps[:, 0:P], wch[c][:].rearrange("p s j -> p (s j)")[:, sl * P:(sl + 1) * P], ident[:]
-            )
-            hl = work.tile([P, 2 * P], BF16, tag="w2hl", bufs=2, name="w2hl")
-            nc.scalar.copy(out=hl[:, 0:P], in_=ps[:, 0:P])
-            w2ps[n] = (ps, hl)
+            ps = psum.tile([P, 512], F32, tag="mx", bufs=3, name="w2ps")
+            for a in range(4):
+                nc.tensor.transpose(
+                    ps[:, a * P:(a + 1) * P],
+                    wch[c][:].rearrange("p s j -> p (s j)")[:, (sl + a) * P:(sl + a + 1) * P],
+                    ident[:],
+                )
+            t = work.tile([P, 512], F32, tag="w2sb", bufs=2, name="w2sb")
+            nc.scalar.copy(out=t[:], in_=ps[:])
+            for a in range(4):
+                w2ps[n + a] = t[:, a * P:(a + 1) * P]
 
         def build_wmix(n):
-            ps, hl = w2ps[n]
-            nc.vector.tensor_tensor(out=hl[:, P:2 * P], in0=ps[:, 0:P], in1=hl[:, 0:P], op=ALU.subtract)
-            wm = work.tile([P, 2 * D], BF16, tag="wm", bufs=2, name="wm")
-            wmv = wm[:].rearrange("p (a s i) -> p a s i", s=SPT, i=NV)
-            src = hl[:].rearrange("p (a i) -> p a i", i=NV)
-            for s in range(SPT):
-                nc.vector.tensor_scalar(
-                    out=wmv[:, :, s, :], in0=src, scalar1=mask[:, s:s + 1], scalar2=None, op0=ALU.mult
-                )
+            wm = work.tile([P, D], F32, tag="wm", bufs=1, name="wm")
+            shp = [P, H, SPT, NV]
+            nc.vector.tensor_tensor(
+                out=wm[:].rearrange("p (h s i) -> p h s i", h=H, s=SPT),
+                in0=w2ps[n].rearrange("p (h i) -> p h i", i=NV).unsqueeze(2).to_broadcast(shp),
+                in1=mask[:].unsqueeze(1).unsqueeze(3).to_broadcast(shp),
+                op=ALU.mult,
+            )
             wmix[n] = wm
 
-        def mix(n, after_first):
-            mb = work.tile([P, D], BF16, tag="mb", bufs=2, name="mb")
-            vh, vl = vsb[n]
+        def mix(n):
+            mt = work.tile([P, D], BF16, tag="mt", bufs=2, name="mt")
+            v = vsb[n]
             wm = wmix[n]
             for q in range(NQ):
-                ps = psum.tile([P, 512], F32, tag="mx", bufs=2, name="mxps")
+                ps = psum.tile([P, 512], F32, tag="mx", bufs=3, name="mxps")
                 for hl in range(4):
                     h = 4 * q + hl
-                    o = ps[:, hl * P:(hl + 1) * P]
-                    hs = slice(h * P, (h + 1) * P)
-                    ls = slice(D + h * P, D + (h + 1) * P)
-                    nc.tensor.matmul(out=o, lhsT=wm[:, hs], rhs=vh[:, hs], start=True, stop=False)
-                    nc.tensor.matmul(out=o, lhsT=wm[:, hs], rhs=vl[:, hs], start=False, stop=False)
-                    nc.tensor.matmul(out=o, lhsT=wm[:, ls], rhs=vh[:, hs], start=False, stop=True)
+                    nc.tensor.matmul(
+                        out=ps[:, hl * P:(hl + 1) * P],
+                        lhsT=v[:, h * P:(h + 1) * P],
+                        rhs=wm[:, h * P:(h + 1) * P],
+                        start=True,
+                        stop=True,
+                    )
                 nc.vector.tensor_tensor(
-                    out=mb[:, q * 512:(q + 1) * 512].rearrange("p (u m e) -> p m u e", u=2, e=2),
-                    in0=ps[:].rearrange("p (m u e) -> p m u e", u=2, e=2),
-                    in1=bv_bc[:, q * 512:(q + 1) * 512].rearrange("p (m u e) -> p m u e", u=2, e=2),
+                    out=mt[:, q * 512:(q + 1) * 512].rearrange("p (a c) -> p a c", a=4),
+                    in0=ps[:].rearrange("p (a c) -> p a c", a=4),
+                    in1=bvT[:, 4 * q:4 * q + 4].unsqueeze(2).to_broadcast([P, 4, P]),
                     op=ALU.add,
                 )
-                if q == 0:
-                    after_first()
-            mbf[n] = mb
+            mtl[n] = mt
 
-        def transp_m(n):
-            mq[n] = to_grouped(mbf[n])
+        def shuffle(n):
+            mt = mtl[n]
+            g0 = work.tile([P, D], BF16, tag="g0", bufs=2, name="g0")
+            for t in range(4):
+                for a in range(4):
+                    nc.sync.dma_start(
+                        out=g0[32 * a:32 * a + 32, :].rearrange("p (g t c) -> p g t c", g=NG, t=4)[:, :, t, :],
+                        in_=mt[t:P:4, :].rearrange("p (g a c) -> p g a c", g=NG, a=4)[:, :, a, :],
+                    )
+            g0l[n] = g0
+
+        def ilv(n):
+            grp = work.tile([P, D], BF16, tag="grp", bufs=3, name="mgrp", align_bytes=64)
+            nc.scalar.copy(
+                out=grp[:].rearrange("p (g c t) -> p g c t", g=NG, t=4),
+                in_=g0l[n][:].rearrange("p (g t c) -> p g c t", g=NG, t=4),
+            )
+            mq[n] = grp
 
         def quant_m(n):
             mq[n] = quantize(mq[n], "mq", LAG + 1)
@@ -296,12 +314,18 @@ def tile_crossviewattention_pa_l_kernel(tc, x, scores, Wv, bv, Wo, bo, out):
         for c in range(W_AHEAD):
             w_load(c)
         load_x(1)
+        nc.vector.memset(bv_rows[:], 0.0)
+        nc.sync.dma_start(out=bv_rows[0:H, :], in_=bv.rearrange("(h c) -> h c", c=P))
         sort_x(0)
         transp_x(0)
         quant_x(0)
         for op in range(6):
             softmax_op(0, op)
         w2t(0)
+        nc.vector.tensor_copy(out=bv_f[:], in_=bv_rows[:])
+        bvps = psum.tile([P, 512], F32, tag="mx", bufs=3, name="bvps")
+        nc.tensor.transpose(bvps[:, 0:P], bv_f[:], ident[:])
+        nc.vector.tensor_copy(out=bvT[:], in_=bvps[:, 0:H])
         for c in range(NQ * NG):
             w_step(c)
             if c == 3:
@@ -311,7 +335,6 @@ def tile_crossviewattention_pa_l_kernel(tc, x, scores, Wv, bv, Wo, bo, out):
                 load_x(2)
             if c == 7:
                 load_x(3)
-                nc.sync.dma_start(out=bv_bc[:], in_=bv.partition_broadcast(P))
             if c == 9:
                 sort_x(2)
             if c == 11:
@@ -332,14 +355,20 @@ def tile_crossviewattention_pa_l_kernel(tc, x, scores, Wv, bv, Wo, bo, out):
                         softmax_op(cnext, k % TPC)
                     if cnext == S // CH - 1 and k % TPC == 2:
                         load_scores(1)
+            if k + 2 < NT:
+                transp_x(k + 2)
+            if k % 4 == 3 and k + 1 < NT:
+                w2t(k + 1)
             if 1 <= k <= NT:
-                transp_m(k - 1)
+                ilv(k - 1)
+            if k + 3 < NT:
+                sort_x(k + 3)
+            if k + 4 < NT:
+                load_x(k + 4)
             if k < NT:
-                if k >= 1:
-                    mix(k, lambda: quant_m(k - 1))
-                else:
-                    mix(k, nothing)
-            elif k == NT:
+                mix(k)
+                shuffle(k)
+            if 1 <= k <= NT:
                 quant_m(k - 1)
             for rep in range(W_PER_ITER):
                 if wnext[0] < len(wchunks):
@@ -347,14 +376,6 @@ def tile_crossviewattention_pa_l_kernel(tc, x, scores, Wv, bv, Wo, bo, out):
                     wnext[0] += 1
                     if wnext[0] == len(wchunks):
                         w_flush()
-            if k + 2 < NT:
-                transp_x(k + 2)
-            if k + 1 < NT:
-                w2t(k + 1)
-            if k + 3 < NT:
-                sort_x(k + 3)
-            if k + 4 < NT:
-                load_x(k + 4)
             if k >= LAG:
                 if k + 2 < NT:
                     stage2(k - LAG, lambda: quant_x(k + 2))

@@ -159,23 +159,28 @@ def tile_crossviewattention_pa_l_kernel(tc, x, scores, Wv, bv, Wo, bo, out):
                 )
                 wch[c] = w
 
-        def to_grouped(src):
-            words = src[:].bitcast(F32)
-            grp = work.tile([P, D], BF16, tag="grp", bufs=3, name="grp", align_bytes=64)
-            gw = grp[:].bitcast(F32).rearrange("p (g r u) -> p g r u", g=NG, u=2)
-            for half in range(2):
-                ps = psum.tile([P, 512], F32, tag="tr", bufs=2, name="trps")
-                for gl in range(2):
-                    g = 2 * half + gl
-                    for u in range(2):
-                        col = (2 * gl + u) * P
-                        lo = 256 * g + P * u
-                        nc.tensor.transpose(ps[:, col:col + P], words[:, lo:lo + P], ident[:])
+        def grouped_step(st, j):
+            half, r4 = divmod(j, 4)
+            if j == 0:
+                st["grp"] = work.tile([P, D], BF16, tag="grp", bufs=3, name="grp", align_bytes=64)
+            if r4 == 0:
+                st["ps"] = psum.tile([P, 512], F32, tag="tr", bufs=2, name="trps")
+            ps = st["ps"]
+            words = st["src"][:].bitcast(F32)
+            lo = 512 * half + P * r4
+            nc.tensor.transpose(ps[:, r4 * P:(r4 + 1) * P], words[:, lo:lo + P], ident[:])
+            if r4 == 3:
+                gw = st["grp"][:].bitcast(F32).rearrange("p (g r u) -> p g r u", g=NG, u=2)
                 nc.scalar.copy(
                     out=gw[:, 2 * half:2 * half + 2, :, :],
                     in_=ps[:].rearrange("p (g u r) -> p g r u", g=2, u=2),
                 )
-            return grp
+
+        def to_grouped(src):
+            st = {"src": src}
+            for j in range(8):
+                grouped_step(st, j)
+            return st["grp"]
 
         def quantize(grp, tag, bufs):
             codes = work.tile([P, 512], U32, tag=tag + "c", bufs=bufs, name=tag + "c", align_bytes=64)
@@ -248,7 +253,7 @@ def tile_crossviewattention_pa_l_kernel(tc, x, scores, Wv, bv, Wo, bo, out):
             )
             wmix[n] = wm
 
-        def mix(n):
+        def mix(n, between, after_first):
             mt = work.tile([P, D], BF16, tag="mt", bufs=2, name="mt")
             v = vsb[n]
             wm = wmix[n]
@@ -263,12 +268,15 @@ def tile_crossviewattention_pa_l_kernel(tc, x, scores, Wv, bv, Wo, bo, out):
                         start=True,
                         stop=True,
                     )
+                    between(h)
                 nc.vector.tensor_tensor(
                     out=mt[:, q * 512:(q + 1) * 512].rearrange("p (a c) -> p a c", a=4),
                     in0=ps[:].rearrange("p (a c) -> p a c", a=4),
                     in1=bvT[:, 4 * q:4 * q + 4].unsqueeze(2).to_broadcast([P, 4, P]),
                     op=ALU.add,
                 )
+                if q == 0:
+                    after_first()
             mtl[n] = mt
 
         def shuffle(n):
@@ -355,27 +363,30 @@ def tile_crossviewattention_pa_l_kernel(tc, x, scores, Wv, bv, Wo, bo, out):
                         softmax_op(cnext, k % TPC)
                     if cnext == S // CH - 1 and k % TPC == 2:
                         load_scores(1)
-            if k + 2 < NT:
-                transp_x(k + 2)
-            if k % 4 == 3 and k + 1 < NT:
-                w2t(k + 1)
-            if 1 <= k <= NT:
-                ilv(k - 1)
             if k + 3 < NT:
                 sort_x(k + 3)
             if k + 4 < NT:
                 load_x(k + 4)
             if k < NT:
-                mix(k)
+                xst = {}
+                if k + 2 < NT:
+                    xst["src"] = xsort[k + 2]
+
+                def between(h):
+                    if h % 2 == 1 and k + 2 < NT:
+                        grouped_step(xst, h // 2)
+                    if h == 11 and k % 4 == 3 and k + 1 < NT:
+                        w2t(k + 1)
+
+                if k >= 2:
+                    mix(k, between, lambda: quant_m(k - 2))
+                else:
+                    mix(k, between, nothing)
+                if k + 2 < NT:
+                    xq[k + 2] = xst["grp"]
                 shuffle(k)
             if 1 <= k <= NT:
-                quant_m(k - 1)
-            for rep in range(W_PER_ITER):
-                if wnext[0] < len(wchunks):
-                    w_step(wnext[0])
-                    wnext[0] += 1
-                    if wnext[0] == len(wchunks):
-                        w_flush()
+                ilv(k - 1)
             if k >= LAG:
                 if k + 2 < NT:
                     stage2(k - LAG, lambda: quant_x(k + 2))
@@ -383,3 +394,11 @@ def tile_crossviewattention_pa_l_kernel(tc, x, scores, Wv, bv, Wo, bo, out):
                     stage2(k - LAG, nothing)
             elif k + 2 < NT:
                 quant_x(k + 2)
+            if NT <= k <= NT + 1:
+                quant_m(k - 2)
+            for rep in range(W_PER_ITER):
+                if wnext[0] < len(wchunks):
+                    w_step(wnext[0])
+                    wnext[0] += 1
+                    if wnext[0] == len(wchunks):
+                        w_flush()

@@ -373,7 +373,7 @@ def tile_crossviewattention_pa_l_kernel(tc, x, scores, Wv, bv, Wo, bo, out):
                     xst["src"] = xsort[k + 2]
 
                 def between(h):
-                    if h % 2 == 1 and k + 2 < NT:
+                    if h % 2 == 0 and k + 2 < NT:
                         grouped_step(xst, h // 2)
                     if h == 11 and k % 4 == 3 and k + 1 < NT:
                         w2t(k + 1)

from contextlib import ExitStack

import concourse.mybir as mybir
from concourse.masks import make_identity

F32 = mybir.dt.float32
BF16 = mybir.dt.bfloat16
U32 = mybir.dt.uint32
U8 = mybir.dt.uint8
FP8X4 = mybir.dt.float8_e4m3fn_x4
ALU = mybir.AluOpType
ACTF = mybir.ActivationFunctionType
AX = mybir.AxisListType

B, NV, S, D, H = 2, 8, 512, 2048, 16
P = 128
SPT = P // NV
NSB = S // SPT
NT = B * NSB
NG = D // 512
NQ = D // 512
CH = 128
TPC = CH // SPT
NCH = B * S // CH

FLOPS = 2 * 2 * B * NV * S * D * D + 2 * B * NV * NV * S * D

LAG = 5
W_AHEAD = 2
W_PER_ITER = 4
RAW_BUFS = 5


def tile_crossviewattention_pa_l_kernel(tc, x, scores, Wv, bv, Wo, bo, out):
    nc = tc.nc
    with ExitStack() as ctx:
        const = ctx.enter_context(tc.tile_pool(name="const", bufs=1))
        work = ctx.enter_context(tc.tile_pool(name="work", bufs=2))
        psum = ctx.enter_context(tc.psum_pool(name="psum", bufs=2))
        ctx.enter_context(tc.manual_schedule())

        warm = const.tile([P, 1], F32, name="warm")
        nc.vector.memset(warm[:], 0.0)
        nc.scalar.activation(out=warm[:], in_=warm[:], func=ACTF.Exp)

        ident = const.tile([P, P], F32, name="ident")
        make_identity(nc, ident[:])
        mask = const.tile([P, SPT], F32, name="mask")
        nc.vector.tensor_reduce(
            out=mask[:], in_=ident[:].rearrange("p (s v) -> p s v", v=NV), axis=AX.X, op=ALU.add
        )

        wv_c = const.tile([P, NG * D], U32, name="wv_c", align_bytes=64)
        wv_s = const.tile([P, NG * D], U8, name="wv_s", align_bytes=64)
        wo_c = const.tile([P, NG * D], U32, name="wo_c", align_bytes=64)
        wo_s = const.tile([P, NG * D], U8, name="wo_s", align_bytes=64)
        bv_rows = const.tile([P, P], BF16, name="bv_rows")
        bv_f = const.tile([P, P], F32, name="bv_f")
        bvT = const.tile([P, H], F32, name="bvT")
        bo_bc = const.tile([P, D], BF16, name="bo_bc")

        xraw = {}
        xsort = {}
        xq = {}
        vsb = {}
        wmix = {}
        w2ps = {}
        mtl = {}
        g0l = {}
        mq = {}
        sct = {}
        sm = {}
        wch = {}

        def load_scores(b):
            t = work.tile([P, NV, S], BF16, tag="sc", bufs=1, name="sc")
            for i in range(NV):
                nc.sync.dma_start(out=t[i:P:NV, :, :], in_=scores[b, i].rearrange("j h s -> h j s"))
            sct[b] = t

        def load_x(n):
            b, sb = divmod(n, NSB)
            t = work.tile([P, D], BF16, tag="raw", bufs=RAW_BUFS, name="xraw")
            for j in range(NV):
                nc.sync.dma_start(out=t[j:P:NV, :], in_=x[b * NV + j, sb * SPT:(sb + 1) * SPT, :])
            xraw[n] = t

        wchunks = []
        for (W, wc, ws) in ((Wv, wv_c, wv_s), (Wo, wo_c, wo_s)):
            for q in range(NQ):
                for g in range(NG):
                    wchunks.append((W, wc, ws, g, q))
        wraw = {}
        wpend = [None]

        def w_load(c):
            W, wc, ws, g, q = wchunks[c]
            t = work.tile([P, D], BF16, tag="raw", bufs=RAW_BUFS, name="wraw")
            nc.sync.dma_start(
                out=t[:].rearrange("p (j c) -> p j c", j=4),
                in_=W.rearrange("(g p j) c -> g p j c", g=NG, j=4)[g, :, :, q * 512:(q + 1) * 512],
            )
            wraw[c] = t

        def w_flush():
            if wpend[0] is not None:
                gt, c = wpend[0]
                W, wc, ws, g, q = wchunks[c]
                lo = g * D + q * 512
                nc.vector.quantize_mx(
                    out=wc[:, lo:lo + 512].bitcast(FP8X4), scales=ws[:, lo:lo + 512], in_=gt[:]
                )
            wpend[0] = None

        def w_step(c):
            gt = work.tile([P, D], BF16, tag="grp", bufs=3, name="wgrp", align_bytes=64)
            o = gt[:].rearrange("p (c j) -> p c j", j=4)
            i = wraw[c][:].rearrange("p (j c) -> p c j", j=4)
            if c % 2 == 0:
                nc.vector.tensor_copy(out=o, in_=i)
            else:
                nc.scalar.copy(out=o, in_=i)
            if c + W_AHEAD < len(wchunks):
                w_load(c + W_AHEAD)
            w_flush()
            wpend[0] = (gt, c)

        def softmax_op(c, op):
            b, qc = divmod(c, S // CH)
            if op == 0:
                src = sct[b][:, :, qc * CH:(qc + 1) * CH].rearrange("p j s -> p s j")
                mxv = work.tile([P, CH], F32, tag="mxv", bufs=1, name="mxv")
                nc.vector.tensor_reduce(out=mxv[:], in_=src, axis=AX.X, op=ALU.max)
                sm[(c, "mx")] = mxv
            elif op == 1:
                src = sct[b][:, :, qc * CH:(qc + 1) * CH].rearrange("p j s -> p s j")
                d = work.tile([P, CH, NV], F32, tag="d", bufs=1, name="d")
                nc.vector.tensor_tensor(
                    out=d[:], in0=src, in1=sm[(c, "mx")][:].unsqueeze(2).to_broadcast([P, CH, NV]),
                    op=ALU.subtract,
                )
                sm[(c, "d")] = d
            elif op == 2:
                d = sm[(c, "d")]
                nc.scalar.activation(out=d[:], in_=d[:], func=ACTF.Exp)
            elif op == 3:
                z = work.tile([P, CH], F32, tag="z", bufs=1, name="z")
                nc.vector.tensor_reduce(out=z[:], in_=sm[(c, "d")][:], axis=AX.X, op=ALU.add)
                sm[(c, "z")] = z
            elif op == 4:
                r = work.tile([P, CH], F32, tag="r", bufs=1, name="r")
                nc.vector.reciprocal(out=r[:], in_=sm[(c, "z")][:])
                sm[(c, "r")] = r
            elif op == 5:
                w = work.tile([P, CH, NV], F32, tag="w", bufs=2, name="w")
                nc.vector.tensor_tensor(
                    out=w[:], in0=sm[(c, "d")][:],
                    in1=sm[(c, "r")][:].unsqueeze(2).to_broadcast([P, CH, NV]), op=ALU.mult,
                )
                wch[c] = w

        def grouped_step(st, j):
            half, r4 = divmod(j, 4)
            if j == 0:
                st["grp"] = work.tile([P, D], BF16, tag="grp", bufs=3, name="grp", align_bytes=64)
            if r4 == 0:
                st["ps"] = psum.tile([P, 512], F32, tag="tr", bufs=2, name="trps")
            ps = st["ps"]
            words = st["src"][:].bitcast(F32)
            lo = 512 * half + P * r4
            nc.tensor.transpose(ps[:, r4 * P:(r4 + 1) * P], words[:, lo:lo + P], ident[:])
            if r4 == 3:
                gw = st["grp"][:].bitcast(F32).rearrange("p (g r u) -> p g r u", g=NG, u=2)
                nc.scalar.copy(
                    out=gw[:, 2 * half:2 * half + 2, :, :],
                    in_=ps[:].rearrange("p (g u r) -> p g r u", g=2, u=2),
                )

        def to_grouped(src):
            st = {"src": src}
            for j in range(8):
                grouped_step(st, j)
            return st["grp"]

        def quantize(grp, tag, bufs):
            codes = work.tile([P, 512], U32, tag=tag + "c", bufs=bufs, name=tag + "c", align_bytes=64)
            scl = work.tile([P, 512], U8, tag=tag + "s", bufs=bufs, name=tag + "s", align_bytes=64)
            nc.vector.quantize_mx(out=codes[:].bitcast(FP8X4), scales=scl[:], in_=grp[:])
            return (codes, scl)

        def mx_stage(opnd, wc, ws, consume):
            codes, scl = opnd
            for q in range(NQ):
                acc = psum.tile([P, 512], F32, tag="acc", bufs=3, name="acc")
                for g in range(NG):
                    lo = g * D + q * 512
                    nc.tensor.matmul_mx(
                        out=acc[:],
                        lhsT=codes[:, g * P:(g + 1) * P].bitcast(FP8X4),
                        lhsT_scale=scl[:, g * P:(g + 1) * P],
                        rhs=wc[:, lo:lo + 512].bitcast(FP8X4),
                        rhs_scale=ws[:, lo:lo + 512],
                        start=(g == 0),
                        stop=(g == NG - 1),
                    )
                consume(q, acc)

        def sort_x(n):
            t = work.tile([P, D], BF16, tag="xs", bufs=2, name="xs")
            nc.scalar.copy(
                out=t[:].bitcast(F32).rearrange("p (g u m) -> p g u m", g=NG, u=2),
                in_=xraw[n][:].bitcast(F32).rearrange("p (g m u) -> p g u m", g=NG, u=2),
            )
            xsort[n] = t

        def transp_x(n):
            xq[n] = to_grouped(xsort[n])

        def quant_x(n):
            xq[n] = quantize(xq[n], "xq", 3)

        def stage1(n):
            v = work.tile([P, D], F32, tag="v", bufs=2, name="v")
            vsb[n] = v

            def consume(q, acc):
                nc.scalar.copy(out=v[:, q * 512:(q + 1) * 512], in_=acc[:])

            mx_stage(xq[n], wv_c, wv_s, consume)

        def w2t(n):
            c, sl = divmod(n, TPC)
            ps = psum.tile([P, 512], F32, tag="mx", bufs=3, name="w2ps")
            for a in range(4):
                nc.tensor.transpose(
                    ps[:, a * P:(a + 1) * P],
                    wch[c][:].rearrange("p s j -> p (s j)")[:, (sl + a) * P:(sl + a + 1) * P],
                    ident[:],
                )
            t = work.tile([P, 512], F32, tag="w2sb", bufs=2, name="w2sb")
            nc.scalar.copy(out=t[:], in_=ps[:])
            for a in range(4):
                w2ps[n + a] = t[:, a * P:(a + 1) * P]

        def build_wmix(n):
            wm = work.tile([P, D], F32, tag="wm", bufs=1, name="wm")
            shp = [P, H, SPT, NV]
            nc.vector.tensor_tensor(
                out=wm[:].rearrange("p (h s i) -> p h s i", h=H, s=SPT),
                in0=w2ps[n].rearrange("p (h i) -> p h i", i=NV).unsqueeze(2).to_broadcast(shp),
                in1=mask[:].unsqueeze(1).unsqueeze(3).to_broadcast(shp),
                op=ALU.mult,
            )
            wmix[n] = wm

        def mix(n, between, after_first):
            mt = work.tile([P, D], BF16, tag="mt", bufs=2, name="mt")
            v = vsb[n]
            wm = wmix[n]
            for q in range(NQ):
                ps = psum.tile([P, 512], F32, tag="mx", bufs=3, name="mxps")
                for hl in range(4):
                    h = 4 * q + hl
                    nc.tensor.matmul(
                        out=ps[:, hl * P:(hl + 1) * P],
                        lhsT=v[:, h * P:(h + 1) * P],
                        rhs=wm[:, h * P:(h + 1) * P],
                        start=True,
                        stop=True,
                    )
                    between(h)
                nc.vector.tensor_tensor(
                    out=mt[:, q * 512:(q + 1) * 512].rearrange("p (a c) -> p a c", a=4),
                    in0=ps[:].rearrange("p (a c) -> p a c", a=4),
                    in1=bvT[:, 4 * q:4 * q + 4].unsqueeze(2).to_broadcast([P, 4, P]),
                    op=ALU.add,
                )
                if q == 0:
                    after_first()
            mtl[n] = mt

        def shuffle(n):
            mt = mtl[n]
            g0 = work.tile([P, D], BF16, tag="g0", bufs=2, name="g0")
            for t in range(4):
                for a in range(4):
                    nc.sync.dma_start(
                        out=g0[32 * a:32 * a + 32, :].rearrange("p (g t c) -> p g t c", g=NG, t=4)[:, :, t, :],
                        in_=mt[t:P:4, :].rearrange("p (g a c) -> p g a c", g=NG, a=4)[:, :, a, :],
                    )
            g0l[n] = g0

        def ilv(n):
            grp = work.tile([P, D], BF16, tag="grp", bufs=3, name="mgrp", align_bytes=64)
            nc.scalar.copy(
                out=grp[:].rearrange("p (g c t) -> p g c t", g=NG, t=4),
                in_=g0l[n][:].rearrange("p (g t c) -> p g c t", g=NG, t=4),
            )
            mq[n] = grp

        def quant_m(n):
            mq[n] = quantize(mq[n], "mq", LAG + 1)

        def stage2(n, after_first):
            b, sb = divmod(n, NSB)
            y = work.tile([P, D], F32, tag="y", bufs=2, name="y")

            def consume(q, acc):
                nc.vector.tensor_tensor(
                    out=y[:, q * 512:(q + 1) * 512], in0=acc[:], in1=bo_bc[:, q * 512:(q + 1) * 512],
                    op=ALU.add,
                )
                if q == 0:
                    after_first()

            mx_stage(mq[n], wo_c, wo_s, consume)
            for i in range(NV):
                nc.sync.dma_start(out=out[b * NV + i, sb * SPT:(sb + 1) * SPT, :], in_=y[i:P:NV, :])

        load_scores(0)
        load_x(0)
        for c in range(W_AHEAD):
            w_load(c)
        load_x(1)
        nc.vector.memset(bv_rows[:], 0.0)
        nc.sync.dma_start(out=bv_rows[0:H, :], in_=bv.rearrange("(h c) -> h c", c=P))
        sort_x(0)
        transp_x(0)
        quant_x(0)
        for op in range(6):
            softmax_op(0, op)
        w2t(0)
        nc.vector.tensor_copy(out=bv_f[:], in_=bv_rows[:])
        bvps = psum.tile([P, 512], F32, tag="mx", bufs=3, name="bvps")
        nc.tensor.transpose(bvps[:, 0:P], bv_f[:], ident[:])
        nc.vector.tensor_copy(out=bvT[:], in_=bvps[:, 0:H])
        for c in range(NQ * NG):
            w_step(c)
            if c == 3:
                sort_x(1)
                transp_x(1)
                quant_x(1)
                load_x(2)
            if c == 7:
                load_x(3)
            if c == 9:
                sort_x(2)
            if c == 11:
                nc.sync.dma_start(out=bo_bc[:], in_=bo.partition_broadcast(P))
        w_flush()

        def nothing():
            return None

        wnext = [NQ * NG]
        for k in range(NT + LAG):
            if k < NT:
                build_wmix(k)
                stage1(k)
                cnext = k // TPC + 1
                if cnext < NCH:
                    if k % TPC < 6:
                        softmax_op(cnext, k % TPC)
                    if cnext == S // CH - 1 and k % TPC == 2:
                        load_scores(1)
            if k + 3 < NT:
                sort_x(k + 3)
            if k + 4 < NT:
                load_x(k + 4)
            if k < NT:
                xst = {}
                if k + 2 < NT:
                    xst["src"] = xsort[k + 2]

                def between(h):
                    if h % 2 == 0 and k + 2 < NT:
                        grouped_step(xst, h // 2)
                    if h == 11 and k % 4 == 3 and k + 1 < NT:
                        w2t(k + 1)

                if k >= 2:
                    mix(k, between, lambda: quant_m(k - 2))
                else:
                    mix(k, between, nothing)
                if k + 2 < NT:
                    xq[k + 2] = xst["grp"]
                shuffle(k)
            if 1 <= k <= NT:
                ilv(k - 1)
            if k >= LAG:
                if k + 2 < NT:
                    stage2(k - LAG, lambda: quant_x(k + 2))
                else:
                    stage2(k - LAG, nothing)
            elif k + 2 < NT:
                quant_x(k + 2)
            if NT <= k <= NT + 1:
                quant_m(k - 2)
            for rep in range(W_PER_ITER):
                if wnext[0] < len(wchunks):
                    w_step(wnext[0])
                    wnext[0] += 1
                    if wnext[0] == len(wchunks):
                        w_flush()
